import numpy as np
import ml_dtypes


def mxq(x, axis, fmt="e4m3"):
    dtype, down = {"e4m3": (ml_dtypes.float8_e4m3fn, 7), "e5m2": (ml_dtypes.float8_e5m2, 14)}[fmt]
    v = np.moveaxis(np.asarray(x, np.float32).astype(ml_dtypes.bfloat16).astype(np.float64), axis, -1)
    blocks = v.reshape(v.shape[:-1] + (-1, 32))
    amax = np.abs(blocks).max(-1, keepdims=True)
    byte = np.maximum(np.where(amax > 0, np.frexp(amax)[1] - 1 + 127, 0) - down, 1)
    scale = np.exp2(byte - 127.0)
    codes = (blocks / scale).astype(np.float32).astype(dtype).astype(np.float64)
    return np.moveaxis((codes * scale).reshape(v.shape), -1, axis)


WIDE = False


def mx_kscale(k):
    if not WIDE:
        return np.ones(k)
    levels = np.array([10, -10, 5, -5, 0])
    a = np.random.permutation(np.resize(levels, k // 512 * 4)).reshape(k // 512, 4)
    idx = np.arange(k)
    return np.exp2(a[idx // 512, idx % 128 // 32])


BF16 = ml_dtypes.bfloat16


def bf(x):
    return np.asarray(x, np.float32).astype(BF16)


def f64(x):
    return np.asarray(x).astype(np.float64)


E2M1 = np.array([0.0, 0.5, 1.0, 1.5, 2.0, 3.0, 4.0, 6.0, -0.0, -0.5, -1.0, -1.5, -2.0, -3.0, -4.0, -6.0])


def pack_weight(w, fmt):
    k, n = w.shape
    w = f64(bf(w)).reshape(k // 32, 32, n)
    amax = np.abs(w).max(1)
    if fmt == "e4m3":
        byte = np.frexp(amax)[1] - 1 + 127 - 7
    else:
        mant, ex = np.frexp(amax / 6.0)
        byte = np.where(mant > 0.5, ex, ex - 1) + 127
    byte = np.clip(np.where(amax > 0, byte, 1), 1, 254)
    scaled = (w * np.exp2(127.0 - byte)[:, None, :]).reshape(k, n).astype(np.float32)
    by_word = np.ascontiguousarray(scaled.reshape(k // 512, 128, 4, n).transpose(0, 1, 3, 2))
    if fmt == "e4m3":
        words = by_word.astype(ml_dtypes.float8_e4m3fn).view(np.uint8)
    else:
        c = by_word.astype(ml_dtypes.float4_e2m1fn).view(np.uint8) & 0xF
        words = c[..., 0::2] | (c[..., 1::2] << 4)
    return np.ascontiguousarray(words), np.ascontiguousarray(byte.astype(np.uint8).reshape(k // 512, 16, n))


def unpack_weight(words, scales, fmt):
    g, p, n, _ = words.shape
    if fmt == "e4m3":
        vals = np.ascontiguousarray(words).view(ml_dtypes.float8_e4m3fn).astype(np.float64)
    else:
        nib = np.empty((g, p, n, 4), np.uint8)
        nib[..., 0::2] = words & 0xF
        nib[..., 1::2] = words >> 4
        vals = E2M1[nib]
    vals = vals * np.repeat(np.exp2(scales.astype(np.float64) - 127.0), 8, axis=1)[..., None]
    return vals.transpose(0, 1, 3, 2).reshape(g * 512, n)

def pack4(w):
    words, scales = pack_weight(w, "e2m1")
    return words.reshape(words.shape[0], 128, -1), scales


def unpack4(words, scales):
    return unpack_weight(words.reshape(words.shape[0], 128, -1, 2), scales, "e2m1")


B, C, T, E, H = 1, 32, 4, 1024, 8
D = E // H
S = C * T


def heads(y):
    return np.moveaxis(y.reshape(B, C, T, H, D), 3, 1)


def setup_inputs():
    s = mx_kscale(E)
    hidden_states = bf(np.random.standard_normal((B, S, E)) * s)
    wk_words, wk_scales = pack4((np.random.standard_normal((E, E)) * 2.0 / np.sqrt(E) / s[None, :]).T)
    bk = bf(np.random.standard_normal(E) * 0.3)
    wv_words, wv_scales = pack4((np.random.standard_normal((E, E)) * 2.0 / np.sqrt(E) / s[None, :]).T)
    bv = bf(np.random.standard_normal(E) * 0.3)
    return {"hidden_states": hidden_states,
            "wk_words": wk_words,
            "wk_scales": wk_scales,
            "bk": bk,
            "wv_words": wv_words,
            "wv_scales": wv_scales,
            "bv": bv}


def reference(hidden_states, wk_words, wk_scales, bk, wv_words, wv_scales, bv):
    xq = mxq(f64(hidden_states), 2, "e4m3")
    k = heads((xq @ unpack4(wk_words, wk_scales)) + f64(bk))
    v = heads((xq @ unpack4(wv_words, wv_scales)) + f64(bv))
    return k, v, k.mean(axis=3), v.mean(axis=3)

@@ -1,0 +1,136 @@
+from contextlib import ExitStack
+
+import concourse.mybir as mybir
+from concourse.masks import make_identity
+
+F32 = mybir.dt.float32
+BF16 = mybir.dt.bfloat16
+I32 = mybir.dt.int32
+U32 = mybir.dt.uint32
+U8 = mybir.dt.uint8
+FP8X4 = mybir.dt.float8_e4m3fn_x4
+FP4X4 = mybir.dt.float4_e2m1fn_x4
+ADD = mybir.AluOpType.add
+
+P = 128
+PACK = 4
+PASSES = 2
+HEADS = 8
+CHUNK = 4
+CHUNKS = P // CHUNK
+BANK_HEADS = 4
+HALVES = HEADS // BANK_HEADS
+FP4_WORD_BYTES = 2
+
+FLOPS = 2 * P * (P * PACK * PASSES) * (2 * HEADS * P)
+
+
+def tile_chunkedattention_pb_s_kernel(
+    tc, hidden_states, wk_words, wk_scales, bk, wv_words, wv_scales, bv, k_out, v_out, k_means_out, v_means_out
+):
+    nc = tc.nc
+    weight_words = (wk_words, wv_words)
+    weight_scales = (wk_scales, wv_scales)
+    biases = (bk, bv)
+    full_outs = [o.rearrange("b h c t d -> (c t) (b h) d") for o in (k_out, v_out)]
+    mean_outs = [o.rearrange("b (f h) c d -> (h c) (b f) d", h=BANK_HEADS) for o in (k_means_out, v_means_out)]
+
+    with ExitStack() as ctx:
+        ctx.enter_context(tc.manual_schedule())
+        keep = ctx.enter_context(tc.tile_pool(name="keep", bufs=1))
+        psum = ctx.enter_context(tc.psum_pool(name="psum", bufs=8))
+
+        x_sb = keep.tile([P, PASSES * P * PACK], BF16)
+        words = [keep.tile([P, PASSES, HEADS * P * FP4_WORD_BYTES], U8, name="words%d" % w, align_bytes=64) for w in range(2)]
+        planes = [keep.tile([P, PASSES, HEADS * P], U8, name="planes%d" % w, align_bytes=64) for w in range(2)]
+        bias_rows = keep.tile([P, P], BF16)
+        bias_cols = keep.tile([P, 2 * HEADS], F32)
+        ident_f32 = keep.tile([P, P], F32)
+        ident_bf16 = keep.tile([P, P], BF16)
+        grouped = keep.tile([P, PASSES, P, PACK], BF16, align_bytes=64)
+        x_codes = keep.tile([P, PASSES * P], U32, align_bytes=64)
+        x_planes = keep.tile([P, PASSES * P], U8, align_bytes=64)
+        by_feature = [keep.tile([P, HEADS, P], F32, name="by_feature%d" % w) for w in range(2)]
+        chunk_sums = [keep.tile([P, HALVES, BANK_HEADS, CHUNKS], F32, name="chunk_sums%d" % w) for w in range(2)]
+        by_token = [keep.tile([P, HEADS, P], F32, name="by_token%d" % w) for w in range(2)]
+        means = [keep.tile([P, HALVES, P], F32, name="means%d" % w) for w in range(2)]
+
+        nc.vector.memset(planes[0][:].bitcast(I32), 0)
+        nc.vector.memset(bias_rows[:], 0.0)
+        nc.vector.memset(planes[1][:].bitcast(I32), 0)
+        make_identity(nc, ident_f32[:])
+        make_identity(nc, ident_bf16[:])
+
+        nc.sync.dma_start(out=x_sb[:], in_=hidden_states.rearrange("b s e -> (b s) e"))
+        for w in range(2):
+            nc.sync.dma_start(out=words[w][:].bitcast(I32), in_=weight_words[w].rearrange("g p b -> p g b").bitcast(I32))
+            rows = weight_scales[w].rearrange("g (q r) n -> r q g n", r=4)
+            for r in range(4):
+                nc.sync.dma_start(out=planes[w][r:P:32].bitcast(I32), in_=rows[r].bitcast(I32))
+            nc.scalar.dma_start(out=bias_rows[HEADS * w : HEADS * (w + 1), :], in_=biases[w].rearrange("(h d) -> h d", d=P))
+
+        x_pairs = x_sb[:].bitcast(F32)
+        pairs_in_pass = P * PACK // 2
+        for g in range(PASSES):
+            turned = psum.tile([P, 2, P], F32, tag="bank")
+            for u in range(2):
+                nc.tensor.transpose(turned[:, u, :], x_pairs[:, pairs_in_pass * g + u : pairs_in_pass * (g + 1) : 2], ident_f32[:])
+            copy = nc.vector.tensor_copy if g == 0 else nc.scalar.copy
+            copy(out=grouped[:, g, :, :].bitcast(F32), in_=turned[:].rearrange("p u s -> p s u"))
+        nc.vector.quantize_mx(
+            out=x_codes[:].bitcast(FP8X4), scales=x_planes[:], in_=grouped[:].rearrange("p g s t -> p (g s t)")
+        )
+
+        bias_turned = psum.tile([P, P], BF16, tag="bank")
+        nc.tensor.transpose(bias_turned[:], bias_rows[:], ident_bf16[:])
+        nc.vector.tensor_copy(out=bias_cols[:], in_=bias_turned[:, 0 : 2 * HEADS])
+
+        for w in range(2):
+            for f in range(HALVES):
+                acc = psum.tile([P, BANK_HEADS, P], F32, tag="bank")
+                for i in range(BANK_HEADS):
+                    h = BANK_HEADS * f + i
+                    for g in range(PASSES):
+                        nc.tensor.matmul_mx(
+                            out=acc[:, i, :],
+                            lhsT=words[w][:, g, P * FP4_WORD_BYTES * h : P * FP4_WORD_BYTES * (h + 1)].bitcast(FP4X4),
+                            lhsT_scale=planes[w][:, g, P * h : P * (h + 1)],
+                            rhs=x_codes[:, P * g : P * (g + 1)].bitcast(FP8X4),
+                            rhs_scale=x_planes[:, P * g : P * (g + 1)],
+                            start=(g == 0),
+                            stop=(g == PASSES - 1),
+                        )
+                heads = slice(BANK_HEADS * f, BANK_HEADS * (f + 1))
+                first = HEADS * w + BANK_HEADS * f
+                nc.vector.tensor_tensor(
+                    out=by_feature[w][:, heads, :],
+                    in0=acc[:],
+                    in1=bias_cols[:, first : first + BANK_HEADS].unsqueeze(2).to_broadcast([P, BANK_HEADS, P]),
+                    op=ADD,
+                )
+                nc.vector.tensor_reduce(
+                    out=chunk_sums[w][:, f, :, :],
+                    in_=by_feature[w][:, heads, :].rearrange("p h (c t) -> p h c t", t=CHUNK),
+                    axis=mybir.AxisListType.X,
+                    op=ADD,
+                )
+
+        for w in range(2):
+            for f in range(HALVES):
+                heads = slice(BANK_HEADS * f, BANK_HEADS * (f + 1))
+                turned_back = psum.tile([P, BANK_HEADS, P], F32, tag="bank")
+                for i in range(BANK_HEADS):
+                    nc.tensor.transpose(turned_back[:, i, :], by_feature[w][:, BANK_HEADS * f + i, :], ident_f32[:])
+                if w == 1 and f == HALVES - 1:
+                    nc.vector.tensor_copy(out=by_token[w][:, heads, :], in_=turned_back[:])
+                else:
+                    nc.scalar.copy(out=by_token[w][:, heads, :], in_=turned_back[:])
+                nc.sync.dma_start(out=full_outs[w][:, heads, :], in_=by_token[w][:, heads, :])
+            sums_turned = psum.tile([P, HALVES, P], F32, tag="bank")
+            for f in range(HALVES):
+                nc.tensor.transpose(sums_turned[:, f, :], chunk_sums[w][:, f, :, :].rearrange("p h c -> p (h c)"), ident_f32[:])
+            if w == 1:
+                nc.vector.tensor_scalar_mul(out=means[w][:], in0=sums_turned[:], scalar1=1.0 / CHUNK)
+            else:
+                nc.scalar.mul(out=means[w][:], in_=sums_turned[:], mul=1.0 / CHUNK)
+            nc.sync.dma_start(out=mean_outs[w], in_=means[w][:])

@@ -32,8 +32,8 @@ def tile_chunkedattention_pb_s_kernel(
     weight_words = (wk_words, wv_words)
     weight_scales = (wk_scales, wv_scales)
     biases = (bk, bv)
-    full_outs = [o.rearrange("b h c t d -> (c t) (b h) d") for o in (k_out, v_out)]
-    mean_outs = [o.rearrange("b (f h) c d -> (h c) (b f) d", h=BANK_HEADS) for o in (k_means_out, v_means_out)]
+    full_outs = [o.rearrange("b (f i) c t d -> f (b i c) (t d)", i=BANK_HEADS) for o in (k_out, v_out)]
+    mean_outs = [o.rearrange("b (f i) c d -> (i c) (b f) d", i=BANK_HEADS) for o in (k_means_out, v_means_out)]
 
     with ExitStack() as ctx:
         ctx.enter_context(tc.manual_schedule())
@@ -50,9 +50,9 @@ def tile_chunkedattention_pb_s_kernel(
         grouped = keep.tile([P, PASSES, P, PACK], BF16, align_bytes=64)
         x_codes = keep.tile([P, PASSES * P], U32, align_bytes=64)
         x_planes = keep.tile([P, PASSES * P], U8, align_bytes=64)
-        by_feature = [keep.tile([P, HEADS, P], F32, name="by_feature%d" % w) for w in range(2)]
+        by_feature = [keep.tile([P, HALVES, CHUNK, BANK_HEADS, CHUNKS], F32, name="by_feature%d" % w) for w in range(2)]
         chunk_sums = [keep.tile([P, HALVES, BANK_HEADS, CHUNKS], F32, name="chunk_sums%d" % w) for w in range(2)]
-        by_token = [keep.tile([P, HEADS, P], F32, name="by_token%d" % w) for w in range(2)]
+        by_chunk = [keep.tile([P, HALVES, CHUNK, P], F32, name="by_chunk%d" % w) for w in range(2)]
         means = [keep.tile([P, HALVES, P], F32, name="means%d" % w) for w in range(2)]
 
         nc.vector.memset(planes[0][:].bitcast(I32), 0)
@@ -76,7 +76,10 @@ def tile_chunkedattention_pb_s_kernel(
             for u in range(2):
                 nc.tensor.transpose(turned[:, u, :], x_pairs[:, pairs_in_pass * g + u : pairs_in_pass * (g + 1) : 2], ident_f32[:])
             copy = nc.vector.tensor_copy if g == 0 else nc.scalar.copy
-            copy(out=grouped[:, g, :, :].bitcast(F32), in_=turned[:].rearrange("p u s -> p s u"))
+            copy(
+                out=grouped[:, g, :, :].bitcast(F32).rearrange("p (t c) u -> p t c u", t=CHUNK),
+                in_=turned[:].rearrange("p u (c t) -> p t c u", t=CHUNK),
+            )
         nc.vector.quantize_mx(
             out=x_codes[:].bitcast(FP8X4), scales=x_planes[:], in_=grouped[:].rearrange("p g s t -> p (g s t)")
         )
@@ -100,35 +103,36 @@ def tile_chunkedattention_pb_s_kernel(
                             start=(g == 0),
                             stop=(g == PASSES - 1),
                         )
-                heads = slice(BANK_HEADS * f, BANK_HEADS * (f + 1))
                 first = HEADS * w + BANK_HEADS * f
                 nc.vector.tensor_tensor(
-                    out=by_feature[w][:, heads, :],
-                    in0=acc[:],
-                    in1=bias_cols[:, first : first + BANK_HEADS].unsqueeze(2).to_broadcast([P, BANK_HEADS, P]),
+                    out=by_feature[w][:, f],
+                    in0=acc[:].rearrange("p i (t c) -> p t i c", t=CHUNK),
+                    in1=bias_cols[:, first : first + BANK_HEADS]
+                    .unsqueeze(1)
+                    .unsqueeze(3)
+                    .to_broadcast([P, CHUNK, BANK_HEADS, CHUNKS]),
                     op=ADD,
                 )
                 nc.vector.tensor_reduce(
-                    out=chunk_sums[w][:, f, :, :],
-                    in_=by_feature[w][:, heads, :].rearrange("p h (c t) -> p h c t", t=CHUNK),
+                    out=chunk_sums[w][:, f],
+                    in_=by_feature[w][:, f].rearrange("p t i c -> p i c t"),
                     axis=mybir.AxisListType.X,
                     op=ADD,
                 )
 
         for w in range(2):
             for f in range(HALVES):
-                heads = slice(BANK_HEADS * f, BANK_HEADS * (f + 1))
-                turned_back = psum.tile([P, BANK_HEADS, P], F32, tag="bank")
-                for i in range(BANK_HEADS):
-                    nc.tensor.transpose(turned_back[:, i, :], by_feature[w][:, BANK_HEADS * f + i, :], ident_f32[:])
+                turned_back = psum.tile([P, CHUNK, P], F32, tag="bank")
+                for t in range(CHUNK):
+                    nc.tensor.transpose(turned_back[:, t, :], by_feature[w][:, f, t].rearrange("p i c -> p (i c)"), ident_f32[:])
                 if w == 1 and f == HALVES - 1:
-                    nc.vector.tensor_copy(out=by_token[w][:, heads, :], in_=turned_back[:])
+                    nc.vector.tensor_copy(out=by_chunk[w][:, f], in_=turned_back[:])
                 else:
-                    nc.scalar.copy(out=by_token[w][:, heads, :], in_=turned_back[:])
-                nc.sync.dma_start(out=full_outs[w][:, heads, :], in_=by_token[w][:, heads, :])
+                    nc.scalar.copy(out=by_chunk[w][:, f], in_=turned_back[:])
+                nc.sync.dma_start(out=full_outs[w][f], in_=by_chunk[w][:, f].rearrange("p t d -> p (t d)"))
             sums_turned = psum.tile([P, HALVES, P], F32, tag="bank")
             for f in range(HALVES):
-                nc.tensor.transpose(sums_turned[:, f, :], chunk_sums[w][:, f, :, :].rearrange("p h c -> p (h c)"), ident_f32[:])
+                nc.tensor.transpose(sums_turned[:, f, :], chunk_sums[w][:, f].rearrange("p i c -> p (i c)"), ident_f32[:])
             if w == 1:
                 nc.vector.tensor_scalar_mul(out=means[w][:], in0=sums_turned[:], scalar1=1.0 / CHUNK)
             else:

@@ -11,6 +11,7 @@ U8 = mybir.dt.uint8
 FP8X4 = mybir.dt.float8_e4m3fn_x4
 FP4X4 = mybir.dt.float4_e2m1fn_x4
 ADD = mybir.AluOpType.add
+IDENTITY = mybir.ActivationFunctionType.Identity
 
 P = 128
 PACK = 4
@@ -21,6 +22,9 @@ CHUNKS = P // CHUNK
 BANK_HEADS = 4
 HALVES = HEADS // BANK_HEADS
 FP4_WORD_BYTES = 2
+IDLE_COLUMNS = 256
+IDLE_BEFORE = 2
+IDLE_AFTER = 2
 
 FLOPS = 2 * P * (P * PACK * PASSES) * (2 * HEADS * P)
 
@@ -32,8 +36,9 @@ def tile_chunkedattention_pb_s_kernel(
     weight_words = (wk_words, wv_words)
     weight_scales = (wk_scales, wv_scales)
     biases = (bk, bv)
-    full_outs = [o.rearrange("b (f i) c t d -> f (b i c) (t d)", i=BANK_HEADS) for o in (k_out, v_out)]
+    full_outs = [o.rearrange("b h c t d -> (c t) (b h) d") for o in (k_out, v_out)]
     mean_outs = [o.rearrange("b (f i) c d -> (i c) (b f) d", i=BANK_HEADS) for o in (k_means_out, v_means_out)]
+    banks = [(w, f) for w in range(2) for f in range(HALVES)]
 
     with ExitStack() as ctx:
         ctx.enter_context(tc.manual_schedule())
@@ -43,6 +48,7 @@ def tile_chunkedattention_pb_s_kernel(
         x_sb = keep.tile([P, PASSES * P * PACK], BF16)
         words = [keep.tile([P, PASSES, HEADS * P * FP4_WORD_BYTES], U8, name="words%d" % w, align_bytes=64) for w in range(2)]
         planes = [keep.tile([P, PASSES, HEADS * P], U8, name="planes%d" % w, align_bytes=64) for w in range(2)]
+        zeros = keep.tile([P, IDLE_COLUMNS], F32)
         bias_rows = keep.tile([P, P], BF16)
         bias_cols = keep.tile([P, 2 * HEADS], F32)
         ident_f32 = keep.tile([P, P], F32)
@@ -50,24 +56,39 @@ def tile_chunkedattention_pb_s_kernel(
         grouped = keep.tile([P, PASSES, P, PACK], BF16, align_bytes=64)
         x_codes = keep.tile([P, PASSES * P], U32, align_bytes=64)
         x_planes = keep.tile([P, PASSES * P], U8, align_bytes=64)
-        by_feature = [keep.tile([P, HALVES, CHUNK, BANK_HEADS, CHUNKS], F32, name="by_feature%d" % w) for w in range(2)]
+        by_feature = [keep.tile([P, HEADS, P], F32, name="by_feature%d" % w) for w in range(2)]
         chunk_sums = [keep.tile([P, HALVES, BANK_HEADS, CHUNKS], F32, name="chunk_sums%d" % w) for w in range(2)]
-        by_chunk = [keep.tile([P, HALVES, CHUNK, P], F32, name="by_chunk%d" % w) for w in range(2)]
+        by_token = [keep.tile([P, HEADS, P], F32, name="by_token%d" % w) for w in range(2)]
         means = [keep.tile([P, HALVES, P], F32, name="means%d" % w) for w in range(2)]
 
-        nc.vector.memset(planes[0][:].bitcast(I32), 0)
+        nc.vector.memset(zeros[:], 0.0)
         nc.vector.memset(bias_rows[:], 0.0)
+        nc.vector.memset(planes[0][:].bitcast(I32), 0)
         nc.vector.memset(planes[1][:].bitcast(I32), 0)
         make_identity(nc, ident_f32[:])
-        make_identity(nc, ident_bf16[:])
+        nc.vector.tensor_copy(out=ident_bf16[:], in_=ident_f32[:])
 
-        nc.sync.dma_start(out=x_sb[:], in_=hidden_states.rearrange("b s e -> (b s) e"))
         for w in range(2):
-            nc.sync.dma_start(out=words[w][:].bitcast(I32), in_=weight_words[w].rearrange("g p b -> p g b").bitcast(I32))
+            nc.scalar.dma_start(out=bias_rows[HEADS * w : HEADS * (w + 1), :], in_=biases[w].rearrange("(h d) -> h d", d=P))
+        nc.sync.dma_start(out=x_sb[:], in_=hidden_states.rearrange("b s e -> (b s) e"))
+
+        def load_scales(w):
             rows = weight_scales[w].rearrange("g (q r) n -> r q g n", r=4)
             for r in range(4):
                 nc.sync.dma_start(out=planes[w][r:P:32].bitcast(I32), in_=rows[r].bitcast(I32))
-            nc.scalar.dma_start(out=bias_rows[HEADS * w : HEADS * (w + 1), :], in_=biases[w].rearrange("(h d) -> h d", d=P))
+
+        load_scales(0)
+        for w in range(2):
+            nc.sync.dma_start(out=words[w][:].bitcast(I32), in_=weight_words[w].rearrange("g p b -> p g b").bitcast(I32))
+        load_scales(1)
+
+        idle_products = psum.tile([P, IDLE_COLUMNS], F32, tag="bank")
+
+        def idle_matmuls(count):
+            for n in range(count):
+                nc.tensor.matmul(out=idle_products[:], lhsT=zeros[:, 0:P], rhs=zeros[:], start=True, stop=True)
+
+        idle_matmuls(IDLE_BEFORE)
 
         x_pairs = x_sb[:].bitcast(F32)
         pairs_in_pass = P * PACK // 2
@@ -76,65 +97,70 @@ def tile_chunkedattention_pb_s_kernel(
             for u in range(2):
                 nc.tensor.transpose(turned[:, u, :], x_pairs[:, pairs_in_pass * g + u : pairs_in_pass * (g + 1) : 2], ident_f32[:])
             copy = nc.vector.tensor_copy if g == 0 else nc.scalar.copy
-            copy(
-                out=grouped[:, g, :, :].bitcast(F32).rearrange("p (t c) u -> p t c u", t=CHUNK),
-                in_=turned[:].rearrange("p u (c t) -> p t c u", t=CHUNK),
-            )
+            copy(out=grouped[:, g, :, :].bitcast(F32), in_=turned[:].rearrange("p u s -> p s u"))
         nc.vector.quantize_mx(
-            out=x_codes[:].bitcast(FP8X4), scales=x_planes[:], in_=grouped[:].rearrange("p g s t -> p (g s t)")
+            out=x_codes[:].bitcast(FP8X4), scales=x_planes[:], in_=grouped[:].rearrange("p g s j -> p (g s j)")
         )
 
         bias_turned = psum.tile([P, P], BF16, tag="bank")
         nc.tensor.transpose(bias_turned[:], bias_rows[:], ident_bf16[:])
         nc.vector.tensor_copy(out=bias_cols[:], in_=bias_turned[:, 0 : 2 * HEADS])
+        idle_matmuls(IDLE_AFTER)
 
-        for w in range(2):
-            for f in range(HALVES):
-                acc = psum.tile([P, BANK_HEADS, P], F32, tag="bank")
-                for i in range(BANK_HEADS):
-                    h = BANK_HEADS * f + i
-                    for g in range(PASSES):
-                        nc.tensor.matmul_mx(
-                            out=acc[:, i, :],
-                            lhsT=words[w][:, g, P * FP4_WORD_BYTES * h : P * FP4_WORD_BYTES * (h + 1)].bitcast(FP4X4),
-                            lhsT_scale=planes[w][:, g, P * h : P * (h + 1)],
-                            rhs=x_codes[:, P * g : P * (g + 1)].bitcast(FP8X4),
-                            rhs_scale=x_planes[:, P * g : P * (g + 1)],
-                            start=(g == 0),
-                            stop=(g == PASSES - 1),
-                        )
-                first = HEADS * w + BANK_HEADS * f
+        def sum_chunks(w, f):
+            heads = slice(BANK_HEADS * f, BANK_HEADS * (f + 1))
+            nc.vector.tensor_reduce(
+                out=chunk_sums[w][:, f],
+                in_=by_feature[w][:, heads, :].rearrange("p i (c t) -> p i c t", t=CHUNK),
+                axis=mybir.AxisListType.X,
+                op=ADD,
+            )
+
+        for b, (w, f) in enumerate(banks):
+            acc = psum.tile([P, BANK_HEADS, P], F32, tag="bank")
+            for i in range(BANK_HEADS):
+                h = BANK_HEADS * f + i
+                for g in range(PASSES):
+                    nc.tensor.matmul_mx(
+                        out=acc[:, i, :],
+                        lhsT=words[w][:, g, P * FP4_WORD_BYTES * h : P * FP4_WORD_BYTES * (h + 1)].bitcast(FP4X4),
+                        lhsT_scale=planes[w][:, g, P * h : P * (h + 1)],
+                        rhs=x_codes[:, P * g : P * (g + 1)].bitcast(FP8X4),
+                        rhs_scale=x_planes[:, P * g : P * (g + 1)],
+                        start=(g == 0),
+                        stop=(g == PASSES - 1),
+                    )
+            first = HEADS * w + BANK_HEADS * f
+            if b == 0 or b == len(banks) - 1:
                 nc.vector.tensor_tensor(
-                    out=by_feature[w][:, f],
-                    in0=acc[:].rearrange("p i (t c) -> p t i c", t=CHUNK),
-                    in1=bias_cols[:, first : first + BANK_HEADS]
-                    .unsqueeze(1)
-                    .unsqueeze(3)
-                    .to_broadcast([P, CHUNK, BANK_HEADS, CHUNKS]),
+                    out=by_feature[w][:, BANK_HEADS * f : BANK_HEADS * (f + 1), :],
+                    in0=acc[:],
+                    in1=bias_cols[:, first : first + BANK_HEADS].unsqueeze(2).to_broadcast([P, BANK_HEADS, P]),
                     op=ADD,
                 )
-                nc.vector.tensor_reduce(
-                    out=chunk_sums[w][:, f],
-                    in_=by_feature[w][:, f].rearrange("p t i c -> p i c t"),
-                    axis=mybir.AxisListType.X,
-                    op=ADD,
-                )
+            else:
+                for i in range(BANK_HEADS):
+                    nc.scalar.activation(
+                        out=by_feature[w][:, BANK_HEADS * f + i, :],
+                        in_=acc[:, i, :],
+                        func=IDENTITY,
+                        bias=bias_cols[:, first + i : first + i + 1],
+                        scale=1.0,
+                    )
+            if b > 0:
+                sum_chunks(*banks[b - 1])
+        sum_chunks(*banks[-1])
 
         for w in range(2):
             for f in range(HALVES):
-                turned_back = psum.tile([P, CHUNK, P], F32, tag="bank")
-                for t in range(CHUNK):
-                    nc.tensor.transpose(turned_back[:, t, :], by_feature[w][:, f, t].rearrange("p i c -> p (i c)"), ident_f32[:])
-                if w == 1 and f == HALVES - 1:
-                    nc.vector.tensor_copy(out=by_chunk[w][:, f], in_=turned_back[:])
-                else:
-                    nc.scalar.copy(out=by_chunk[w][:, f], in_=turned_back[:])
-                nc.sync.dma_start(out=full_outs[w][f], in_=by_chunk[w][:, f].rearrange("p t d -> p (t d)"))
+                heads = slice(BANK_HEADS * f, BANK_HEADS * (f + 1))
+                turned_back = psum.tile([P, BANK_HEADS, P], F32, tag="bank")
+                for i in range(BANK_HEADS):
+                    nc.tensor.transpose(turned_back[:, i, :], by_feature[w][:, BANK_HEADS * f + i, :], ident_f32[:])
+                nc.scalar.copy(out=by_token[w][:, heads, :], in_=turned_back[:])
+                nc.sync.dma_start(out=full_outs[w][:, heads, :], in_=by_token[w][:, heads, :])
             sums_turned = psum.tile([P, HALVES, P], F32, tag="bank")
             for f in range(HALVES):
                 nc.tensor.transpose(sums_turned[:, f, :], chunk_sums[w][:, f].rearrange("p i c -> p (i c)"), ident_f32[:])
-            if w == 1:
-                nc.vector.tensor_scalar_mul(out=means[w][:], in0=sums_turned[:], scalar1=1.0 / CHUNK)
-            else:
-                nc.scalar.mul(out=means[w][:], in_=sums_turned[:], mul=1.0 / CHUNK)
+            nc.vector.tensor_scalar_mul(out=means[w][:], in0=sums_turned[:], scalar1=1.0 / CHUNK)
             nc.sync.dma_start(out=mean_outs[w], in_=means[w][:])

@@ -11,7 +11,6 @@ U8 = mybir.dt.uint8
 FP8X4 = mybir.dt.float8_e4m3fn_x4
 FP4X4 = mybir.dt.float4_e2m1fn_x4
 ADD = mybir.AluOpType.add
-IDENTITY = mybir.ActivationFunctionType.Identity
 
 P = 128
 PACK = 4
@@ -20,11 +19,14 @@ HEADS = 8
 CHUNK = 4
 CHUNKS = P // CHUNK
 BANK_HEADS = 4
+BANK = BANK_HEADS * P
 HALVES = HEADS // BANK_HEADS
+FEATURES = HEADS * P
 FP4_WORD_BYTES = 2
+BIAS_WORDS = 4
 IDLE_COLUMNS = 256
 IDLE_BEFORE = 2
-IDLE_AFTER = 2
+IDLE_AFTER = 1
 
 FLOPS = 2 * P * (P * PACK * PASSES) * (2 * HEADS * P)
 
@@ -46,31 +48,29 @@ def tile_chunkedattention_pb_s_kernel(
         psum = ctx.enter_context(tc.psum_pool(name="psum", bufs=8))
 
         x_sb = keep.tile([P, PASSES * P * PACK], BF16)
-        words = [keep.tile([P, PASSES, HEADS * P * FP4_WORD_BYTES], U8, name="words%d" % w, align_bytes=64) for w in range(2)]
-        planes = [keep.tile([P, PASSES, HEADS * P], U8, name="planes%d" % w, align_bytes=64) for w in range(2)]
+        words = [keep.tile([P, PASSES, FEATURES * FP4_WORD_BYTES], U8, name="words%d" % w, align_bytes=64) for w in range(2)]
+        planes = [keep.tile([P, PASSES, FEATURES], U8, name="planes%d" % w, align_bytes=64) for w in range(2)]
         zeros = keep.tile([P, IDLE_COLUMNS], F32)
-        bias_rows = keep.tile([P, P], BF16)
-        bias_cols = keep.tile([P, 2 * HEADS], F32)
-        ident_f32 = keep.tile([P, P], F32)
-        ident_bf16 = keep.tile([P, P], BF16)
+        bias_cols = [keep.tile([P, 2 * BIAS_WORDS], BF16, name="bias_cols%d" % w) for w in range(2)]
+        bias_all = [keep.tile([P, FEATURES // 2], F32, name="bias_all%d" % w) for w in range(2)]
+        ident = keep.tile([P, P], F32)
+        warm = keep.tile([P, 1], F32)
         grouped = keep.tile([P, PASSES, P, PACK], BF16, align_bytes=64)
         x_codes = keep.tile([P, PASSES * P], U32, align_bytes=64)
         x_planes = keep.tile([P, PASSES * P], U8, align_bytes=64)
-        by_feature = [keep.tile([P, HEADS, P], F32, name="by_feature%d" % w) for w in range(2)]
-        chunk_sums = [keep.tile([P, HALVES, BANK_HEADS, CHUNKS], F32, name="chunk_sums%d" % w) for w in range(2)]
-        by_token = [keep.tile([P, HEADS, P], F32, name="by_token%d" % w) for w in range(2)]
-        means = [keep.tile([P, HALVES, P], F32, name="means%d" % w) for w in range(2)]
+        y = [keep.tile([P, FEATURES], F32, name="y%d" % w) for w in range(2)]
+        sums_sb = [keep.tile([P, P], F32, name="sums_sb%d" % b) for b in range(len(banks))]
+        means = [keep.tile([P, P], F32, name="means%d" % b) for b in range(len(banks))]
 
-        nc.vector.memset(zeros[:], 0.0)
-        nc.vector.memset(bias_rows[:], 0.0)
+        nc.gpsimd.memset(zeros[:], 0.0)
         nc.vector.memset(planes[0][:].bitcast(I32), 0)
         nc.vector.memset(planes[1][:].bitcast(I32), 0)
-        make_identity(nc, ident_f32[:])
-        nc.vector.tensor_copy(out=ident_bf16[:], in_=ident_f32[:])
+        make_identity(nc, ident[:])
+        nc.scalar.mul(out=warm[:], in_=zeros[:, 0:1], mul=1.0)
 
-        for w in range(2):
-            nc.scalar.dma_start(out=bias_rows[HEADS * w : HEADS * (w + 1), :], in_=biases[w].rearrange("(h d) -> h d", d=P))
         nc.sync.dma_start(out=x_sb[:], in_=hidden_states.rearrange("b s e -> (b s) e"))
+        for w in range(2):
+            nc.scalar.dma_start(out=bias_cols[w][:], in_=biases[w].rearrange("(n e) -> n e", e=2 * BIAS_WORDS))
 
         def load_scales(w):
             rows = weight_scales[w].rearrange("g (q r) n -> r q g n", r=4)
@@ -92,75 +92,79 @@ def tile_chunkedattention_pb_s_kernel(
 
         x_pairs = x_sb[:].bitcast(F32)
         pairs_in_pass = P * PACK // 2
+        turned = []
         for g in range(PASSES):
-            turned = psum.tile([P, 2, P], F32, tag="bank")
+            turned_g = psum.tile([P, 2, P], F32, tag="bank")
+            turned.append(turned_g)
             for u in range(2):
-                nc.tensor.transpose(turned[:, u, :], x_pairs[:, pairs_in_pass * g + u : pairs_in_pass * (g + 1) : 2], ident_f32[:])
-            copy = nc.vector.tensor_copy if g == 0 else nc.scalar.copy
-            copy(out=grouped[:, g, :, :].bitcast(F32), in_=turned[:].rearrange("p u s -> p s u"))
-        nc.vector.quantize_mx(
-            out=x_codes[:].bitcast(FP8X4), scales=x_planes[:], in_=grouped[:].rearrange("p g s j -> p (g s j)")
-        )
+                nc.tensor.transpose(turned_g[:, u, :], x_pairs[:, pairs_in_pass * g + u : pairs_in_pass * (g + 1) : 2], ident[:])
+        for g in range(PASSES):
+            nc.scalar.copy(out=grouped[:, g, :, :].bitcast(F32), in_=turned[g][:].rearrange("p u s -> p s u"))
+            nc.vector.quantize_mx(
+                out=x_codes[:, P * g : P * (g + 1)].bitcast(FP8X4),
+                scales=x_planes[:, P * g : P * (g + 1)],
+                in_=grouped[:, g, :, :].rearrange("p s j -> p (s j)"),
+            )
 
-        bias_turned = psum.tile([P, P], BF16, tag="bank")
-        nc.tensor.transpose(bias_turned[:], bias_rows[:], ident_bf16[:])
-        nc.vector.tensor_copy(out=bias_cols[:], in_=bias_turned[:, 0 : 2 * HEADS])
+        for w in range(2):
+            spread = psum.tile([P, BIAS_WORDS, P], F32, tag="bank")
+            bias_words = bias_cols[w][:].bitcast(F32)
+            for j in range(BIAS_WORDS):
+                nc.tensor.transpose(spread[:, j, :], bias_words[:, j : j + 1].to_broadcast([P, P]), ident[:])
+            nc.scalar.copy(
+                out=bias_all[w][:].rearrange("p (n j) -> p n j", j=BIAS_WORDS), in_=spread[:].rearrange("p j n -> p n j")
+            )
+
         idle_matmuls(IDLE_AFTER)
 
-        def sum_chunks(w, f):
-            heads = slice(BANK_HEADS * f, BANK_HEADS * (f + 1))
+        def multiply(acc, w, f, g):
+            nc.tensor.matmul_mx(
+                out=acc[:],
+                lhsT=x_codes[:, P * g : P * (g + 1)].bitcast(FP8X4),
+                lhsT_scale=x_planes[:, P * g : P * (g + 1)],
+                rhs=words[w][:, g, BANK * FP4_WORD_BYTES * f : BANK * FP4_WORD_BYTES * (f + 1)].bitcast(FP4X4),
+                rhs_scale=planes[w][:, g, BANK * f : BANK * (f + 1)],
+                start=(g == 0),
+                stop=(g == PASSES - 1),
+            )
+
+        accs = [psum.tile([P, BANK], F32, tag="bank", name="acc%d" % b) for b in range(len(banks))]
+        for g in range(PASSES):
+            for f in range(HALVES):
+                multiply(accs[f], 0, f, g)
+        for f in range(HALVES):
+            for g in range(PASSES):
+                multiply(accs[HALVES + f], 1, f, g)
+
+        for b, (w, f) in enumerate(banks):
+            cols = slice(BANK * f, BANK * (f + 1))
+            nc.vector.tensor_tensor(out=y[w][:, cols], in0=accs[b][:], in1=bias_all[w][:].bitcast(BF16)[:, cols], op=ADD)
+            nc.sync.dma_start(
+                out=full_outs[w][:, BANK_HEADS * f : BANK_HEADS * (f + 1), :],
+                in_=y[w][:, cols].rearrange("p (i d) -> p i d", d=P),
+            )
+
+        def sum_chunks(b):
+            w, f = banks[b]
+            by_feature = psum.tile([P, BANK_HEADS, P], F32, tag="bank")
+            for i in range(BANK_HEADS):
+                h = BANK_HEADS * f + i
+                nc.tensor.transpose(by_feature[:, i, :], y[w][:, P * h : P * (h + 1)], ident[:])
             nc.vector.tensor_reduce(
-                out=chunk_sums[w][:, f],
-                in_=by_feature[w][:, heads, :].rearrange("p i (c t) -> p i c t", t=CHUNK),
+                out=sums_sb[b][:].rearrange("p (i c) -> p i c", c=CHUNKS),
+                in_=by_feature[:].rearrange("p i (c t) -> p i c t", t=CHUNK),
                 axis=mybir.AxisListType.X,
                 op=ADD,
             )
 
-        for b, (w, f) in enumerate(banks):
-            acc = psum.tile([P, BANK_HEADS, P], F32, tag="bank")
-            for i in range(BANK_HEADS):
-                h = BANK_HEADS * f + i
-                for g in range(PASSES):
-                    nc.tensor.matmul_mx(
-                        out=acc[:, i, :],
-                        lhsT=words[w][:, g, P * FP4_WORD_BYTES * h : P * FP4_WORD_BYTES * (h + 1)].bitcast(FP4X4),
-                        lhsT_scale=planes[w][:, g, P * h : P * (h + 1)],
-                        rhs=x_codes[:, P * g : P * (g + 1)].bitcast(FP8X4),
-                        rhs_scale=x_planes[:, P * g : P * (g + 1)],
-                        start=(g == 0),
-                        stop=(g == PASSES - 1),
-                    )
-            first = HEADS * w + BANK_HEADS * f
-            if b == 0 or b == len(banks) - 1:
-                nc.vector.tensor_tensor(
-                    out=by_feature[w][:, BANK_HEADS * f : BANK_HEADS * (f + 1), :],
-                    in0=acc[:],
-                    in1=bias_cols[:, first : first + BANK_HEADS].unsqueeze(2).to_broadcast([P, BANK_HEADS, P]),
-                    op=ADD,
-                )
-            else:
-                for i in range(BANK_HEADS):
-                    nc.scalar.activation(
-                        out=by_feature[w][:, BANK_HEADS * f + i, :],
-                        in_=acc[:, i, :],
-                        func=IDENTITY,
-                        bias=bias_cols[:, first + i : first + i + 1],
-                        scale=1.0,
-                    )
-            if b > 0:
-                sum_chunks(*banks[b - 1])
-        sum_chunks(*banks[-1])
+        def store_means(b):
+            w, f = banks[b]
+            turned_back = psum.tile([P, P], F32, tag="bank")
+            nc.tensor.transpose(turned_back[:], sums_sb[b][:], ident[:])
+            nc.scalar.mul(out=means[b][:], in_=turned_back[:], mul=1.0 / CHUNK)
+            nc.sync.dma_start(out=mean_outs[w][:, f, :], in_=means[b][:])
 
-        for w in range(2):
-            for f in range(HALVES):
-                heads = slice(BANK_HEADS * f, BANK_HEADS * (f + 1))
-                turned_back = psum.tile([P, BANK_HEADS, P], F32, tag="bank")
-                for i in range(BANK_HEADS):
-                    nc.tensor.transpose(turned_back[:, i, :], by_feature[w][:, BANK_HEADS * f + i, :], ident_f32[:])
-                nc.scalar.copy(out=by_token[w][:, heads, :], in_=turned_back[:])
-                nc.sync.dma_start(out=full_outs[w][:, heads, :], in_=by_token[w][:, heads, :])
-            sums_turned = psum.tile([P, HALVES, P], F32, tag="bank")
-            for f in range(HALVES):
-                nc.tensor.transpose(sums_turned[:, f, :], chunk_sums[w][:, f].rearrange("p i c -> p (i c)"), ident_f32[:])
-            nc.vector.tensor_scalar_mul(out=means[w][:], in0=sums_turned[:], scalar1=1.0 / CHUNK)
-            nc.sync.dma_start(out=mean_outs[w], in_=means[w][:])
+        for b in range(len(banks)):
+            sum_chunks(b)
+        for b in range(len(banks)):
+            store_means(b)

@@ -26,7 +26,7 @@ FP4_WORD_BYTES = 2
 BIAS_WORDS = 4
 IDLE_COLUMNS = 256
 IDLE_BEFORE = 2
-IDLE_AFTER = 1
+IDLE_AFTER = 0
 
 FLOPS = 2 * P * (P * PACK * PASSES) * (2 * HEADS * P)
 
@@ -61,26 +61,29 @@ def tile_chunkedattention_pb_s_kernel(
         y = [keep.tile([P, FEATURES], F32, name="y%d" % w) for w in range(2)]
         sums_sb = [keep.tile([P, P], F32, name="sums_sb%d" % b) for b in range(len(banks))]
         means = [keep.tile([P, P], F32, name="means%d" % b) for b in range(len(banks))]
+        by_place = [keep.tile([P, CHUNK, P], F32, name="by_place%d" % b) for b in range(HALVES)]
 
         nc.gpsimd.memset(zeros[:], 0.0)
         nc.vector.memset(planes[0][:].bitcast(I32), 0)
         nc.vector.memset(planes[1][:].bitcast(I32), 0)
         make_identity(nc, ident[:])
-        nc.scalar.mul(out=warm[:], in_=zeros[:, 0:1], mul=1.0)
 
         nc.sync.dma_start(out=x_sb[:], in_=hidden_states.rearrange("b s e -> (b s) e"))
         for w in range(2):
             nc.scalar.dma_start(out=bias_cols[w][:], in_=biases[w].rearrange("(n e) -> n e", e=2 * BIAS_WORDS))
+        nc.scalar.mul(out=warm[:], in_=zeros[:, 0:1], mul=1.0)
 
         def load_scales(w):
             rows = weight_scales[w].rearrange("g (q r) n -> r q g n", r=4)
             for r in range(4):
                 nc.sync.dma_start(out=planes[w][r:P:32].bitcast(I32), in_=rows[r].bitcast(I32))
 
-        load_scales(0)
         for w in range(2):
-            nc.sync.dma_start(out=words[w][:].bitcast(I32), in_=weight_words[w].rearrange("g p b -> p g b").bitcast(I32))
-        load_scales(1)
+            load_scales(w)
+            by_partition = weight_words[w].rearrange("g p b -> p g b")
+            for f in range(HALVES):
+                bank_bytes = slice(BANK * FP4_WORD_BYTES * f, BANK * FP4_WORD_BYTES * (f + 1))
+                nc.sync.dma_start(out=words[w][:, :, bank_bytes].bitcast(I32), in_=by_partition[:, :, bank_bytes].bitcast(I32))
 
         idle_products = psum.tile([P, IDLE_COLUMNS], F32, tag="bank")
 
@@ -129,12 +132,9 @@ def tile_chunkedattention_pb_s_kernel(
             )
 
         accs = [psum.tile([P, BANK], F32, tag="bank", name="acc%d" % b) for b in range(len(banks))]
-        for g in range(PASSES):
-            for f in range(HALVES):
-                multiply(accs[f], 0, f, g)
-        for f in range(HALVES):
+        for b, (w, f) in enumerate(banks):
             for g in range(PASSES):
-                multiply(accs[HALVES + f], 1, f, g)
+                multiply(accs[b], w, f, g)
 
         for b, (w, f) in enumerate(banks):
             cols = slice(BANK * f, BANK * (f + 1))
@@ -144,27 +144,39 @@ def tile_chunkedattention_pb_s_kernel(
                 in_=y[w][:, cols].rearrange("p (i d) -> p i d", d=P),
             )
 
-        def sum_chunks(b):
+        def turn_heads(b):
             w, f = banks[b]
             by_feature = psum.tile([P, BANK_HEADS, P], F32, tag="bank")
             for i in range(BANK_HEADS):
                 h = BANK_HEADS * f + i
                 nc.tensor.transpose(by_feature[:, i, :], y[w][:, P * h : P * (h + 1)], ident[:])
-            nc.vector.tensor_reduce(
-                out=sums_sb[b][:].rearrange("p (i c) -> p i c", c=CHUNKS),
-                in_=by_feature[:].rearrange("p i (c t) -> p i c t", t=CHUNK),
-                axis=mybir.AxisListType.X,
-                op=ADD,
-            )
+            return by_feature
 
-        def store_means(b):
+        def store_means(turned_back, b):
             w, f = banks[b]
-            turned_back = psum.tile([P, P], F32, tag="bank")
-            nc.tensor.transpose(turned_back[:], sums_sb[b][:], ident[:])
             nc.scalar.mul(out=means[b][:], in_=turned_back[:], mul=1.0 / CHUNK)
             nc.sync.dma_start(out=mean_outs[w][:, f, :], in_=means[b][:])
 
+        turned_heads = [turn_heads(b) for b in range(len(banks))]
+        for b in range(HALVES):
+            nc.scalar.copy(
+                out=by_place[b][:].rearrange("p t (i c) -> p t i c", c=CHUNKS),
+                in_=turned_heads[b][:].rearrange("p i (c t) -> p t i c", t=CHUNK),
+            )
+        for b in range(HALVES, len(banks)):
+            nc.vector.tensor_reduce(
+                out=sums_sb[b][:].rearrange("p (i c) -> p i c", c=CHUNKS),
+                in_=turned_heads[b][:].rearrange("p i (c t) -> p i c t", t=CHUNK),
+                axis=mybir.AxisListType.X,
+                op=ADD,
+            )
         for b in range(len(banks)):
-            sum_chunks(b)
-        for b in range(len(banks)):
-            store_means(b)
+            turned_back = psum.tile([P, P], F32, tag="bank")
+            if b < HALVES:
+                for t in range(CHUNK):
+                    nc.tensor.matmul(
+                        out=turned_back[:], lhsT=by_place[b][:, t, :], rhs=ident[:], start=(t == 0), stop=(t == CHUNK - 1), is_transpose=True
+                    )
+            else:
+                nc.tensor.transpose(turned_back[:], sums_sb[b][:], ident[:])
+            store_means(turned_back, b)

@@ -81,9 +81,11 @@ def tile_chunkedattention_pb_s_kernel(
         for w in range(2):
             load_scales(w)
             by_partition = weight_words[w].rearrange("g p b -> p g b")
-            for f in range(HALVES):
-                bank_bytes = slice(BANK * FP4_WORD_BYTES * f, BANK * FP4_WORD_BYTES * (f + 1))
-                nc.sync.dma_start(out=words[w][:, :, bank_bytes].bitcast(I32), in_=by_partition[:, :, bank_bytes].bitcast(I32))
+            pieces = 1 if w == 0 else HALVES
+            piece = FEATURES * FP4_WORD_BYTES // pieces
+            for f in range(pieces):
+                piece_bytes = slice(piece * f, piece * (f + 1))
+                nc.sync.dma_start(out=words[w][:, :, piece_bytes].bitcast(I32), in_=by_partition[:, :, piece_bytes].bitcast(I32))
 
         idle_products = psum.tile([P, IDLE_COLUMNS], F32, tag="bank")
 

@@ -26,7 +26,6 @@ FP4_WORD_BYTES = 2
 BIAS_WORDS = 4
 IDLE_COLUMNS = 256
 IDLE_BEFORE = 2
-IDLE_AFTER = 0
 
 FLOPS = 2 * P * (P * PACK * PASSES) * (2 * HEADS * P)
 
@@ -37,7 +36,6 @@ def tile_chunkedattention_pb_s_kernel(
     nc = tc.nc
     weight_words = (wk_words, wv_words)
     weight_scales = (wk_scales, wv_scales)
-    biases = (bk, bv)
     full_outs = [o.rearrange("b h c t d -> (c t) (b h) d") for o in (k_out, v_out)]
     mean_outs = [o.rearrange("b (f i) c d -> (i c) (b f) d", i=BANK_HEADS) for o in (k_means_out, v_means_out)]
     banks = [(w, f) for w in range(2) for f in range(HALVES)]
@@ -66,11 +64,11 @@ def tile_chunkedattention_pb_s_kernel(
         nc.gpsimd.memset(zeros[:], 0.0)
         nc.vector.memset(planes[0][:].bitcast(I32), 0)
         nc.vector.memset(planes[1][:].bitcast(I32), 0)
-        make_identity(nc, ident[:])
 
         nc.sync.dma_start(out=x_sb[:], in_=hidden_states.rearrange("b s e -> (b s) e"))
-        for w in range(2):
-            nc.scalar.dma_start(out=bias_cols[w][:], in_=biases[w].rearrange("(n e) -> n e", e=2 * BIAS_WORDS))
+        nc.scalar.dma_start(out=bias_cols[0][:], in_=bk.rearrange("(n e) -> n e", e=2 * BIAS_WORDS))
+        make_identity(nc, ident[:])
+        nc.gpsimd.dma_start(out=bias_cols[1][:], in_=bv.rearrange("(n e) -> n e", e=2 * BIAS_WORDS))
         nc.scalar.mul(out=warm[:], in_=zeros[:, 0:1], mul=1.0)
 
         def load_scales(w):
@@ -81,11 +79,13 @@ def tile_chunkedattention_pb_s_kernel(
         for w in range(2):
             load_scales(w)
             by_partition = weight_words[w].rearrange("g p b -> p g b")
-            pieces = 1 if w == 0 else HALVES
-            piece = FEATURES * FP4_WORD_BYTES // pieces
-            for f in range(pieces):
-                piece_bytes = slice(piece * f, piece * (f + 1))
-                nc.sync.dma_start(out=words[w][:, :, piece_bytes].bitcast(I32), in_=by_partition[:, :, piece_bytes].bitcast(I32))
+            if w == 0:
+                for g in range(PASSES):
+                    nc.sync.dma_start(out=words[w][:, g, :].bitcast(I32), in_=by_partition[:, g, :].bitcast(I32))
+            else:
+                for f in range(HALVES):
+                    bank_bytes = slice(BANK * FP4_WORD_BYTES * f, BANK * FP4_WORD_BYTES * (f + 1))
+                    nc.sync.dma_start(out=words[w][:, :, bank_bytes].bitcast(I32), in_=by_partition[:, :, bank_bytes].bitcast(I32))
 
         idle_products = psum.tile([P, IDLE_COLUMNS], F32, tag="bank")
 
@@ -111,7 +111,7 @@ def tile_chunkedattention_pb_s_kernel(
                 in_=grouped[:, g, :, :].rearrange("p s j -> p (s j)"),
             )
 
-        for w in range(2):
+        def spread_bias(w):
             spread = psum.tile([P, BIAS_WORDS, P], F32, tag="bank")
             bias_words = bias_cols[w][:].bitcast(F32)
             for j in range(BIAS_WORDS):
@@ -120,7 +120,7 @@ def tile_chunkedattention_pb_s_kernel(
                 out=bias_all[w][:].rearrange("p (n j) -> p n j", j=BIAS_WORDS), in_=spread[:].rearrange("p j n -> p n j")
             )
 
-        idle_matmuls(IDLE_AFTER)
+        spread_bias(0)
 
         def multiply(acc, w, f, g):
             nc.tensor.matmul_mx(
@@ -134,9 +134,13 @@ def tile_chunkedattention_pb_s_kernel(
             )
 
         accs = [psum.tile([P, BANK], F32, tag="bank", name="acc%d" % b) for b in range(len(banks))]
-        for b, (w, f) in enumerate(banks):
+        for g in range(PASSES):
+            for f in range(HALVES):
+                multiply(accs[f], 0, f, g)
+        spread_bias(1)
+        for f in range(HALVES):
             for g in range(PASSES):
-                multiply(accs[b], w, f, g)
+                multiply(accs[HALVES + f], 1, f, g)
 
         for b, (w, f) in enumerate(banks):
             cols = slice(BANK * f, BANK * (f + 1))

@@ -65,10 +65,10 @@ def tile_chunkedattention_pb_s_kernel(
         nc.vector.memset(planes[0][:].bitcast(I32), 0)
         nc.vector.memset(planes[1][:].bitcast(I32), 0)
 
+        for w, bias in enumerate((bk, bv)):
+            nc.scalar.dma_start(out=bias_cols[w][:], in_=bias.rearrange("(n e) -> n e", e=2 * BIAS_WORDS))
         nc.sync.dma_start(out=x_sb[:], in_=hidden_states.rearrange("b s e -> (b s) e"))
-        nc.scalar.dma_start(out=bias_cols[0][:], in_=bk.rearrange("(n e) -> n e", e=2 * BIAS_WORDS))
         make_identity(nc, ident[:])
-        nc.gpsimd.dma_start(out=bias_cols[1][:], in_=bv.rearrange("(n e) -> n e", e=2 * BIAS_WORDS))
         nc.scalar.mul(out=warm[:], in_=zeros[:, 0:1], mul=1.0)
 
         def load_scales(w):
@@ -121,6 +121,7 @@ def tile_chunkedattention_pb_s_kernel(
             )
 
         spread_bias(0)
+        spread_bias(1)
 
         def multiply(acc, w, f, g):
             nc.tensor.matmul_mx(
@@ -137,7 +138,6 @@ def tile_chunkedattention_pb_s_kernel(
         for g in range(PASSES):
             for f in range(HALVES):
                 multiply(accs[f], 0, f, g)
-        spread_bias(1)
         for f in range(HALVES):
             for g in range(PASSES):
                 multiply(accs[HALVES + f], 1, f, g)

@@ -16,16 +16,18 @@ P = 128
 PACK = 4
 PASSES = 2
 HEADS = 8
+FEATURES = HEADS * P
 CHUNK = 4
 CHUNKS = P // CHUNK
 BANK_HEADS = 4
 BANK = BANK_HEADS * P
 HALVES = HEADS // BANK_HEADS
-FEATURES = HEADS * P
 FP4_WORD_BYTES = 2
+QUADRANT = 32
+SCALE_ROWS = 4
 BIAS_WORDS = 4
 IDLE_COLUMNS = 256
-IDLE_BEFORE = 2
+IDLE_MATMULS = 2
 
 FLOPS = 2 * P * (P * PACK * PASSES) * (2 * HEADS * P)
 
@@ -52,32 +54,29 @@ def tile_chunkedattention_pb_s_kernel(
         bias_cols = [keep.tile([P, 2 * BIAS_WORDS], BF16, name="bias_cols%d" % w) for w in range(2)]
         bias_all = [keep.tile([P, FEATURES // 2], F32, name="bias_all%d" % w) for w in range(2)]
         ident = keep.tile([P, P], F32)
-        warm = keep.tile([P, 1], F32)
+        table_warmer = keep.tile([P, 1], F32)
         grouped = keep.tile([P, PASSES, P, PACK], BF16, align_bytes=64)
         x_codes = keep.tile([P, PASSES * P], U32, align_bytes=64)
         x_planes = keep.tile([P, PASSES * P], U8, align_bytes=64)
         y = [keep.tile([P, FEATURES], F32, name="y%d" % w) for w in range(2)]
-        sums_sb = [keep.tile([P, P], F32, name="sums_sb%d" % b) for b in range(len(banks))]
+        chunk_sums = [keep.tile([P, P], F32, name="chunk_sums%d" % f) for f in range(HALVES)]
         means = [keep.tile([P, P], F32, name="means%d" % b) for b in range(len(banks))]
-        by_place = [keep.tile([P, CHUNK, P], F32, name="by_place%d" % b) for b in range(HALVES)]
+        by_place = [keep.tile([P, CHUNK, P], F32, name="by_place%d" % f) for f in range(HALVES)]
 
         nc.gpsimd.memset(zeros[:], 0.0)
         nc.vector.memset(planes[0][:].bitcast(I32), 0)
         nc.vector.memset(planes[1][:].bitcast(I32), 0)
 
         for w, bias in enumerate((bk, bv)):
-            nc.scalar.dma_start(out=bias_cols[w][:], in_=bias.rearrange("(n e) -> n e", e=2 * BIAS_WORDS))
+            nc.scalar.dma_start(out=bias_cols[w][:], in_=bias.rearrange("(o x) -> o x", x=2 * BIAS_WORDS))
         nc.sync.dma_start(out=x_sb[:], in_=hidden_states.rearrange("b s e -> (b s) e"))
         make_identity(nc, ident[:])
-        nc.scalar.mul(out=warm[:], in_=zeros[:, 0:1], mul=1.0)
-
-        def load_scales(w):
-            rows = weight_scales[w].rearrange("g (q r) n -> r q g n", r=4)
-            for r in range(4):
-                nc.sync.dma_start(out=planes[w][r:P:32].bitcast(I32), in_=rows[r].bitcast(I32))
+        nc.scalar.mul(out=table_warmer[:], in_=zeros[:, 0:1], mul=1.0)
 
         for w in range(2):
-            load_scales(w)
+            rows = weight_scales[w].rearrange("g (quad r) n -> r quad g n", r=SCALE_ROWS)
+            for r in range(SCALE_ROWS):
+                nc.sync.dma_start(out=planes[w][r:P:QUADRANT].bitcast(I32), in_=rows[r].bitcast(I32))
             by_partition = weight_words[w].rearrange("g p b -> p g b")
             if w == 0:
                 for g in range(PASSES):
@@ -88,12 +87,8 @@ def tile_chunkedattention_pb_s_kernel(
                     nc.sync.dma_start(out=words[w][:, :, bank_bytes].bitcast(I32), in_=by_partition[:, :, bank_bytes].bitcast(I32))
 
         idle_products = psum.tile([P, IDLE_COLUMNS], F32, tag="bank")
-
-        def idle_matmuls(count):
-            for n in range(count):
-                nc.tensor.matmul(out=idle_products[:], lhsT=zeros[:, 0:P], rhs=zeros[:], start=True, stop=True)
-
-        idle_matmuls(IDLE_BEFORE)
+        for repeat in range(IDLE_MATMULS):
+            nc.tensor.matmul(out=idle_products[:], lhsT=zeros[:, 0:P], rhs=zeros[:], start=True, stop=True)
 
         x_pairs = x_sb[:].bitcast(F32)
         pairs_in_pass = P * PACK // 2
@@ -111,17 +106,14 @@ def tile_chunkedattention_pb_s_kernel(
                 in_=grouped[:, g, :, :].rearrange("p s j -> p (s j)"),
             )
 
-        def spread_bias(w):
+        for w in range(2):
             spread = psum.tile([P, BIAS_WORDS, P], F32, tag="bank")
             bias_words = bias_cols[w][:].bitcast(F32)
-            for j in range(BIAS_WORDS):
-                nc.tensor.transpose(spread[:, j, :], bias_words[:, j : j + 1].to_broadcast([P, P]), ident[:])
+            for m in range(BIAS_WORDS):
+                nc.tensor.transpose(spread[:, m, :], bias_words[:, m : m + 1].to_broadcast([P, P]), ident[:])
             nc.scalar.copy(
-                out=bias_all[w][:].rearrange("p (n j) -> p n j", j=BIAS_WORDS), in_=spread[:].rearrange("p j n -> p n j")
+                out=bias_all[w][:].rearrange("p (o m) -> p o m", m=BIAS_WORDS), in_=spread[:].rearrange("p m o -> p o m")
             )
-
-        spread_bias(0)
-        spread_bias(1)
 
         def multiply(acc, w, f, g):
             nc.tensor.matmul_mx(
@@ -150,39 +142,33 @@ def tile_chunkedattention_pb_s_kernel(
                 in_=y[w][:, cols].rearrange("p (i d) -> p i d", d=P),
             )
 
-        def turn_heads(b):
-            w, f = banks[b]
-            by_feature = psum.tile([P, BANK_HEADS, P], F32, tag="bank")
+        by_feature = []
+        for w, f in banks:
+            by_feature_b = psum.tile([P, BANK_HEADS, P], F32, tag="bank")
+            by_feature.append(by_feature_b)
             for i in range(BANK_HEADS):
                 h = BANK_HEADS * f + i
-                nc.tensor.transpose(by_feature[:, i, :], y[w][:, P * h : P * (h + 1)], ident[:])
-            return by_feature
-
-        def store_means(turned_back, b):
-            w, f = banks[b]
-            nc.scalar.mul(out=means[b][:], in_=turned_back[:], mul=1.0 / CHUNK)
-            nc.sync.dma_start(out=mean_outs[w][:, f, :], in_=means[b][:])
-
-        turned_heads = [turn_heads(b) for b in range(len(banks))]
-        for b in range(HALVES):
+                nc.tensor.transpose(by_feature_b[:, i, :], y[w][:, P * h : P * (h + 1)], ident[:])
+        for f in range(HALVES):
             nc.scalar.copy(
-                out=by_place[b][:].rearrange("p t (i c) -> p t i c", c=CHUNKS),
-                in_=turned_heads[b][:].rearrange("p i (c t) -> p t i c", t=CHUNK),
+                out=by_place[f][:].rearrange("p t (i c) -> p t i c", c=CHUNKS),
+                in_=by_feature[f][:].rearrange("p i (c t) -> p t i c", t=CHUNK),
             )
-        for b in range(HALVES, len(banks)):
+        for f in range(HALVES):
             nc.vector.tensor_reduce(
-                out=sums_sb[b][:].rearrange("p (i c) -> p i c", c=CHUNKS),
-                in_=turned_heads[b][:].rearrange("p i (c t) -> p i c t", t=CHUNK),
+                out=chunk_sums[f][:].rearrange("p (i c) -> p i c", c=CHUNKS),
+                in_=by_feature[HALVES + f][:].rearrange("p i (c t) -> p i c t", t=CHUNK),
                 axis=mybir.AxisListType.X,
                 op=ADD,
             )
-        for b in range(len(banks)):
+        for b, (w, f) in enumerate(banks):
             turned_back = psum.tile([P, P], F32, tag="bank")
-            if b < HALVES:
+            if w == 0:
                 for t in range(CHUNK):
                     nc.tensor.matmul(
-                        out=turned_back[:], lhsT=by_place[b][:, t, :], rhs=ident[:], start=(t == 0), stop=(t == CHUNK - 1), is_transpose=True
+                        out=turned_back[:], lhsT=by_place[f][:, t, :], rhs=ident[:], start=(t == 0), stop=(t == CHUNK - 1), is_transpose=True
                     )
             else:
-                nc.tensor.transpose(turned_back[:], sums_sb[b][:], ident[:])
-            store_means(turned_back, b)
+                nc.tensor.transpose(turned_back[:], chunk_sums[f][:], ident[:])
+            nc.scalar.mul(out=means[b][:], in_=turned_back[:], mul=1.0 / CHUNK)
+            nc.sync.dma_start(out=mean_outs[w][:, f, :], in_=means[b][:])

@@ -13,7 +13,9 @@ FP4X4 = mybir.dt.float4_e2m1fn_x4
 ADD = mybir.AluOpType.add
 
 P = 128
+PROJECTIONS = 2
 PACK = 4
+PAIRS = PACK // 2
 PASSES = 2
 HEADS = 8
 FEATURES = HEADS * P
@@ -29,7 +31,7 @@ BIAS_WORDS = 4
 IDLE_COLUMNS = 256
 IDLE_MATMULS = 2
 
-FLOPS = 2 * P * (P * PACK * PASSES) * (2 * HEADS * P)
+FLOPS = 2 * P * (P * PACK * PASSES) * (PROJECTIONS * FEATURES)
 
 
 def tile_chunkedattention_pb_s_kernel(
@@ -40,7 +42,7 @@ def tile_chunkedattention_pb_s_kernel(
     weight_scales = (wk_scales, wv_scales)
     full_outs = [o.rearrange("b h c t d -> (c t) (b h) d") for o in (k_out, v_out)]
     mean_outs = [o.rearrange("b (f i) c d -> (i c) (b f) d", i=BANK_HEADS) for o in (k_means_out, v_means_out)]
-    banks = [(w, f) for w in range(2) for f in range(HALVES)]
+    banks = [(w, f) for w in range(PROJECTIONS) for f in range(HALVES)]
 
     with ExitStack() as ctx:
         ctx.enter_context(tc.manual_schedule())
@@ -48,17 +50,17 @@ def tile_chunkedattention_pb_s_kernel(
         psum = ctx.enter_context(tc.psum_pool(name="psum", bufs=8))
 
         x_sb = keep.tile([P, PASSES * P * PACK], BF16)
-        words = [keep.tile([P, PASSES, FEATURES * FP4_WORD_BYTES], U8, name="words%d" % w, align_bytes=64) for w in range(2)]
-        planes = [keep.tile([P, PASSES, FEATURES], U8, name="planes%d" % w, align_bytes=64) for w in range(2)]
+        words = [keep.tile([P, PASSES, FEATURES * FP4_WORD_BYTES], U8, name="words%d" % w, align_bytes=64) for w in range(PROJECTIONS)]
+        planes = [keep.tile([P, PASSES, FEATURES], U8, name="planes%d" % w, align_bytes=64) for w in range(PROJECTIONS)]
         zeros = keep.tile([P, IDLE_COLUMNS], F32)
-        bias_cols = [keep.tile([P, 2 * BIAS_WORDS], BF16, name="bias_cols%d" % w) for w in range(2)]
-        bias_all = [keep.tile([P, FEATURES // 2], F32, name="bias_all%d" % w) for w in range(2)]
+        bias_cols = [keep.tile([P, 2 * BIAS_WORDS], BF16, name="bias_cols%d" % w) for w in range(PROJECTIONS)]
+        bias_all = [keep.tile([P, FEATURES // 2], F32, name="bias_all%d" % w) for w in range(PROJECTIONS)]
         ident = keep.tile([P, P], F32)
         table_warmer = keep.tile([P, 1], F32)
         grouped = keep.tile([P, PASSES, P, PACK], BF16, align_bytes=64)
         x_codes = keep.tile([P, PASSES * P], U32, align_bytes=64)
         x_planes = keep.tile([P, PASSES * P], U8, align_bytes=64)
-        y = [keep.tile([P, FEATURES], F32, name="y%d" % w) for w in range(2)]
+        y = [keep.tile([P, FEATURES], F32, name="y%d" % w) for w in range(PROJECTIONS)]
         chunk_sums = [keep.tile([P, P], F32, name="chunk_sums%d" % f) for f in range(HALVES)]
         means = [keep.tile([P, P], F32, name="means%d" % b) for b in range(len(banks))]
         by_place = [keep.tile([P, CHUNK, P], F32, name="by_place%d" % f) for f in range(HALVES)]
@@ -73,7 +75,7 @@ def tile_chunkedattention_pb_s_kernel(
         make_identity(nc, ident[:])
         nc.scalar.mul(out=table_warmer[:], in_=zeros[:, 0:1], mul=1.0)
 
-        for w in range(2):
+        for w in range(PROJECTIONS):
             rows = weight_scales[w].rearrange("g (quad r) n -> r quad g n", r=SCALE_ROWS)
             for r in range(SCALE_ROWS):
                 nc.sync.dma_start(out=planes[w][r:P:QUADRANT].bitcast(I32), in_=rows[r].bitcast(I32))
@@ -91,13 +93,13 @@ def tile_chunkedattention_pb_s_kernel(
             nc.tensor.matmul(out=idle_products[:], lhsT=zeros[:, 0:P], rhs=zeros[:], start=True, stop=True)
 
         x_pairs = x_sb[:].bitcast(F32)
-        pairs_in_pass = P * PACK // 2
+        pairs_in_pass = P * PAIRS
         turned = []
         for g in range(PASSES):
-            turned_g = psum.tile([P, 2, P], F32, tag="bank")
+            turned_g = psum.tile([P, PAIRS, P], F32, tag="bank")
             turned.append(turned_g)
-            for u in range(2):
-                nc.tensor.transpose(turned_g[:, u, :], x_pairs[:, pairs_in_pass * g + u : pairs_in_pass * (g + 1) : 2], ident[:])
+            for u in range(PAIRS):
+                nc.tensor.transpose(turned_g[:, u, :], x_pairs[:, pairs_in_pass * g + u : pairs_in_pass * (g + 1) : PAIRS], ident[:])
         for g in range(PASSES):
             nc.scalar.copy(out=grouped[:, g, :, :].bitcast(F32), in_=turned[g][:].rearrange("p u s -> p s u"))
             nc.vector.quantize_mx(
@@ -106,7 +108,7 @@ def tile_chunkedattention_pb_s_kernel(
                 in_=grouped[:, g, :, :].rearrange("p s j -> p (s j)"),
             )
 
-        for w in range(2):
+        for w in range(PROJECTIONS):
             spread = psum.tile([P, BIAS_WORDS, P], F32, tag="bank")
             bias_words = bias_cols[w][:].bitcast(F32)
             for m in range(BIAS_WORDS):
@@ -142,10 +144,12 @@ def tile_chunkedattention_pb_s_kernel(
                 in_=y[w][:, cols].rearrange("p (i d) -> p i d", d=P),
             )
 
-        by_feature = []
-        for w, f in banks:
+        by_readiness = (0, 2, 1, 3)
+        by_feature = {}
+        for b in by_readiness:
+            w, f = banks[b]
             by_feature_b = psum.tile([P, BANK_HEADS, P], F32, tag="bank")
-            by_feature.append(by_feature_b)
+            by_feature[b] = by_feature_b
             for i in range(BANK_HEADS):
                 h = BANK_HEADS * f + i
                 nc.tensor.transpose(by_feature_b[:, i, :], y[w][:, P * h : P * (h + 1)], ident[:])
@@ -161,7 +165,8 @@ def tile_chunkedattention_pb_s_kernel(
                 axis=mybir.AxisListType.X,
                 op=ADD,
             )
-        for b, (w, f) in enumerate(banks):
+        for b in by_readiness:
+            w, f = banks[b]
             turned_back = psum.tile([P, P], F32, tag="bank")
             if w == 0:
                 for t in range(CHUNK):
@@ -170,5 +175,8 @@ def tile_chunkedattention_pb_s_kernel(
                     )
             else:
                 nc.tensor.transpose(turned_back[:], chunk_sums[f][:], ident[:])
-            nc.scalar.mul(out=means[b][:], in_=turned_back[:], mul=1.0 / CHUNK)
+            if b == by_readiness[-1]:
+                nc.vector.tensor_scalar_mul(out=means[b][:], in0=turned_back[:], scalar1=1.0 / CHUNK)
+            else:
+                nc.scalar.mul(out=means[b][:], in_=turned_back[:], mul=1.0 / CHUNK)
             nc.sync.dma_start(out=mean_outs[w][:, f, :], in_=means[b][:])

@@ -29,7 +29,7 @@ QUADRANT = 32
 SCALE_ROWS = 4
 BIAS_WORDS = 4
 IDLE_COLUMNS = 256
-IDLE_MATMULS = 2
+IDLE_MATMULS = 1
 
 FLOPS = 2 * P * (P * PACK * PASSES) * (PROJECTIONS * FEATURES)
 
@@ -75,18 +75,17 @@ def tile_chunkedattention_pb_s_kernel(
         make_identity(nc, ident[:])
         nc.scalar.mul(out=table_warmer[:], in_=zeros[:, 0:1], mul=1.0)
 
-        for w in range(PROJECTIONS):
+        def load_scales(w):
             rows = weight_scales[w].rearrange("g (quad r) n -> r quad g n", r=SCALE_ROWS)
             for r in range(SCALE_ROWS):
                 nc.sync.dma_start(out=planes[w][r:P:QUADRANT].bitcast(I32), in_=rows[r].bitcast(I32))
-            by_partition = weight_words[w].rearrange("g p b -> p g b")
-            if w == 0:
-                for g in range(PASSES):
-                    nc.sync.dma_start(out=words[w][:, g, :].bitcast(I32), in_=by_partition[:, g, :].bitcast(I32))
-            else:
-                for f in range(HALVES):
-                    bank_bytes = slice(BANK * FP4_WORD_BYTES * f, BANK * FP4_WORD_BYTES * (f + 1))
-                    nc.sync.dma_start(out=words[w][:, :, bank_bytes].bitcast(I32), in_=by_partition[:, :, bank_bytes].bitcast(I32))
+
+        by_partition = [words_in.rearrange("g p b -> p g b") for words_in in weight_words]
+        nc.sync.dma_start(out=words[0][:, 0, :].bitcast(I32), in_=by_partition[0][:, 0, :].bitcast(I32))
+        load_scales(0)
+        nc.sync.dma_start(out=words[0][:, 1, :].bitcast(I32), in_=by_partition[0][:, 1, :].bitcast(I32))
+        nc.sync.dma_start(out=words[1][:].bitcast(I32), in_=by_partition[1].bitcast(I32))
+        load_scales(1)
 
         idle_products = psum.tile([P, IDLE_COLUMNS], F32, tag="bank")
         for repeat in range(IDLE_MATMULS):

@@ -29,7 +29,7 @@ QUADRANT = 32
 SCALE_ROWS = 4
 BIAS_WORDS = 4
 IDLE_COLUMNS = 256
-IDLE_MATMULS = 1
+IDLE_MATMULS = 2
 
 FLOPS = 2 * P * (P * PACK * PASSES) * (PROJECTIONS * FEATURES)
 

@@ -65,14 +65,15 @@ def tile_chunkedattention_pb_s_kernel(
         means = [keep.tile([P, P], F32, name="means%d" % b) for b in range(len(banks))]
         by_place = [keep.tile([P, CHUNK, P], F32, name="by_place%d" % f) for f in range(HALVES)]
 
-        nc.gpsimd.memset(zeros[:], 0.0)
+        nc.vector.memset(ident[:], 0.0)
         nc.vector.memset(planes[0][:].bitcast(I32), 0)
-        nc.vector.memset(planes[1][:].bitcast(I32), 0)
+        nc.vector.memset(zeros[:], 0.0)
 
         for w, bias in enumerate((bk, bv)):
             nc.scalar.dma_start(out=bias_cols[w][:], in_=bias.rearrange("(o x) -> o x", x=2 * BIAS_WORDS))
         nc.sync.dma_start(out=x_sb[:], in_=hidden_states.rearrange("b s e -> (b s) e"))
-        make_identity(nc, ident[:])
+        make_identity(nc, ident[:], nomemset=True)
+        nc.gpsimd.memset(planes[1][:].bitcast(F32), 0.0)
         nc.scalar.mul(out=table_warmer[:], in_=zeros[:, 0:1], mul=1.0)
 
         def load_scales(w):

@@ -28,7 +28,7 @@ FP4_WORD_BYTES = 2
 QUADRANT = 32
 SCALE_ROWS = 4
 BIAS_WORDS = 4
-IDLE_COLUMNS = 256
+IDLE_COLUMNS = 192
 IDLE_MATMULS = 2
 
 FLOPS = 2 * P * (P * PACK * PASSES) * (PROJECTIONS * FEATURES)
@@ -50,7 +50,7 @@ def tile_chunkedattention_pb_s_kernel(
         psum = ctx.enter_context(tc.psum_pool(name="psum", bufs=8))
 
         x_sb = keep.tile([P, PASSES * P * PACK], BF16)
-        words = [keep.tile([P, PASSES, FEATURES * FP4_WORD_BYTES], U8, name="words%d" % w, align_bytes=64) for w in range(PROJECTIONS)]
+        words = {(w, f): keep.tile([P, PASSES, BANK * FP4_WORD_BYTES], U8, name="words%d%d" % (w, f), align_bytes=64) for w, f in banks}
         planes = [keep.tile([P, PASSES, FEATURES], U8, name="planes%d" % w, align_bytes=64) for w in range(PROJECTIONS)]
         zeros = keep.tile([P, IDLE_COLUMNS], F32)
         bias_cols = [keep.tile([P, 2 * BIAS_WORDS], BF16, name="bias_cols%d" % w) for w in range(PROJECTIONS)]
@@ -65,28 +65,34 @@ def tile_chunkedattention_pb_s_kernel(
         means = [keep.tile([P, P], F32, name="means%d" % b) for b in range(len(banks))]
         by_place = [keep.tile([P, CHUNK, P], F32, name="by_place%d" % f) for f in range(HALVES)]
 
-        nc.vector.memset(ident[:], 0.0)
+        nc.gpsimd.memset(zeros[:], 0.0)
         nc.vector.memset(planes[0][:].bitcast(I32), 0)
-        nc.vector.memset(zeros[:], 0.0)
+        nc.vector.memset(planes[1][:].bitcast(I32), 0)
 
         for w, bias in enumerate((bk, bv)):
             nc.scalar.dma_start(out=bias_cols[w][:], in_=bias.rearrange("(o x) -> o x", x=2 * BIAS_WORDS))
         nc.sync.dma_start(out=x_sb[:], in_=hidden_states.rearrange("b s e -> (b s) e"))
-        make_identity(nc, ident[:], nomemset=True)
-        nc.gpsimd.memset(planes[1][:].bitcast(F32), 0.0)
+        make_identity(nc, ident[:])
         nc.scalar.mul(out=table_warmer[:], in_=zeros[:, 0:1], mul=1.0)
 
-        def load_scales(w):
+        def load_scale_rows(w, r):
             rows = weight_scales[w].rearrange("g (quad r) n -> r quad g n", r=SCALE_ROWS)
-            for r in range(SCALE_ROWS):
-                nc.sync.dma_start(out=planes[w][r:P:QUADRANT].bitcast(I32), in_=rows[r].bitcast(I32))
+            nc.sync.dma_start(out=planes[w][r:P:QUADRANT].bitcast(I32), in_=rows[r].bitcast(I32))
 
-        by_partition = [words_in.rearrange("g p b -> p g b") for words_in in weight_words]
-        nc.sync.dma_start(out=words[0][:, 0, :].bitcast(I32), in_=by_partition[0][:, 0, :].bitcast(I32))
-        load_scales(0)
-        nc.sync.dma_start(out=words[0][:, 1, :].bitcast(I32), in_=by_partition[0][:, 1, :].bitcast(I32))
-        nc.sync.dma_start(out=words[1][:].bitcast(I32), in_=by_partition[1].bitcast(I32))
-        load_scales(1)
+        def load_words(w, f):
+            bank_bytes = slice(BANK * FP4_WORD_BYTES * f, BANK * FP4_WORD_BYTES * (f + 1))
+            by_partition = weight_words[w].rearrange("g p b -> p g b")
+            nc.sync.dma_start(out=words[w, f][:].bitcast(I32), in_=by_partition[:, :, bank_bytes].bitcast(I32))
+
+        for r in range(SCALE_ROWS):
+            load_scale_rows(0, r)
+        for f in range(HALVES):
+            load_words(0, f)
+        load_scale_rows(1, 0)
+        load_words(1, 0)
+        for r in range(1, SCALE_ROWS):
+            load_scale_rows(1, r)
+        load_words(1, 1)
 
         idle_products = psum.tile([P, IDLE_COLUMNS], F32, tag="bank")
         for repeat in range(IDLE_MATMULS):
@@ -122,19 +128,16 @@ def tile_chunkedattention_pb_s_kernel(
                 out=acc[:],
                 lhsT=x_codes[:, P * g : P * (g + 1)].bitcast(FP8X4),
                 lhsT_scale=x_planes[:, P * g : P * (g + 1)],
-                rhs=words[w][:, g, BANK * FP4_WORD_BYTES * f : BANK * FP4_WORD_BYTES * (f + 1)].bitcast(FP4X4),
+                rhs=words[w, f][:, g, :].bitcast(FP4X4),
                 rhs_scale=planes[w][:, g, BANK * f : BANK * (f + 1)],
                 start=(g == 0),
                 stop=(g == PASSES - 1),
             )
 
         accs = [psum.tile([P, BANK], F32, tag="bank", name="acc%d" % b) for b in range(len(banks))]
-        for g in range(PASSES):
-            for f in range(HALVES):
-                multiply(accs[f], 0, f, g)
-        for f in range(HALVES):
+        for b, (w, f) in enumerate(banks):
             for g in range(PASSES):
-                multiply(accs[HALVES + f], 1, f, g)
+                multiply(accs[b], w, f, g)
 
         for b, (w, f) in enumerate(banks):
             cols = slice(BANK * f, BANK * (f + 1))
@@ -145,26 +148,30 @@ def tile_chunkedattention_pb_s_kernel(
             )
 
         by_readiness = (0, 2, 1, 3)
-        by_feature = {}
+        pieces = []
         for b in by_readiness:
             w, f = banks[b]
-            by_feature_b = psum.tile([P, BANK_HEADS, P], F32, tag="bank")
-            by_feature[b] = by_feature_b
-            for i in range(BANK_HEADS):
-                h = BANK_HEADS * f + i
-                nc.tensor.transpose(by_feature_b[:, i, :], y[w][:, P * h : P * (h + 1)], ident[:])
-        for f in range(HALVES):
-            nc.scalar.copy(
-                out=by_place[f][:].rearrange("p t (i c) -> p t i c", c=CHUNKS),
-                in_=by_feature[f][:].rearrange("p i (c t) -> p t i c", t=CHUNK),
-            )
-        for f in range(HALVES):
-            nc.vector.tensor_reduce(
-                out=chunk_sums[f][:].rearrange("p (i c) -> p i c", c=CHUNKS),
-                in_=by_feature[HALVES + f][:].rearrange("p i (c t) -> p i c t", t=CHUNK),
-                axis=mybir.AxisListType.X,
-                op=ADD,
-            )
+            heads = BANK_HEADS if f == 0 else BANK_HEADS // 2
+            for first in range(0, BANK_HEADS, heads):
+                by_feature = psum.tile([P, heads, P], F32, tag="bank")
+                pieces.append((w, f, first, heads, by_feature))
+                for i in range(heads):
+                    h = BANK_HEADS * f + first + i
+                    nc.tensor.transpose(by_feature[:, i, :], y[w][:, P * h : P * (h + 1)], ident[:])
+        for w, f, first, heads, by_feature in pieces:
+            sums = slice(CHUNKS * first, CHUNKS * (first + heads))
+            if w == 0:
+                nc.scalar.copy(
+                    out=by_place[f][:, :, sums].rearrange("p t (i c) -> p t i c", c=CHUNKS),
+                    in_=by_feature[:].rearrange("p i (c t) -> p t i c", t=CHUNK),
+                )
+            else:
+                nc.vector.tensor_reduce(
+                    out=chunk_sums[f][:, sums].rearrange("p (i c) -> p i c", c=CHUNKS),
+                    in_=by_feature[:].rearrange("p i (c t) -> p i c t", t=CHUNK),
+                    axis=mybir.AxisListType.X,
+                    op=ADD,
+                )
         for b in by_readiness:
             w, f = banks[b]
             turned_back = psum.tile([P, P], F32, tag="bank")

from contextlib import ExitStack

import concourse.mybir as mybir
from concourse.masks import make_identity

F32 = mybir.dt.float32
BF16 = mybir.dt.bfloat16
I32 = mybir.dt.int32
U32 = mybir.dt.uint32
U8 = mybir.dt.uint8
FP8X4 = mybir.dt.float8_e4m3fn_x4
FP4X4 = mybir.dt.float4_e2m1fn_x4
ADD = mybir.AluOpType.add

P = 128
PROJECTIONS = 2
PACK = 4
PAIRS = PACK // 2
PASSES = 2
HEADS = 8
FEATURES = HEADS * P
CHUNK = 4
CHUNKS = P // CHUNK
BANK_HEADS = 4
BANK = BANK_HEADS * P
HALVES = HEADS // BANK_HEADS
FP4_WORD_BYTES = 2
QUADRANT = 32
SCALE_ROWS = 4
BIAS_WORDS = 4
IDLE_COLUMNS = 192
IDLE_MATMULS = 2

FLOPS = 2 * P * (P * PACK * PASSES) * (PROJECTIONS * FEATURES)


def tile_chunkedattention_pb_s_kernel(
    tc, hidden_states, wk_words, wk_scales, bk, wv_words, wv_scales, bv, k_out, v_out, k_means_out, v_means_out
):
    nc = tc.nc
    weight_words = (wk_words, wv_words)
    weight_scales = (wk_scales, wv_scales)
    full_outs = [o.rearrange("b h c t d -> (c t) (b h) d") for o in (k_out, v_out)]
    mean_outs = [o.rearrange("b (f i) c d -> (i c) (b f) d", i=BANK_HEADS) for o in (k_means_out, v_means_out)]
    banks = [(w, f) for w in range(PROJECTIONS) for f in range(HALVES)]

    with ExitStack() as ctx:
        ctx.enter_context(tc.manual_schedule())
        keep = ctx.enter_context(tc.tile_pool(name="keep", bufs=1))
        psum = ctx.enter_context(tc.psum_pool(name="psum", bufs=8))

        x_sb = keep.tile([P, PASSES * P * PACK], BF16)
        words = {(w, f): keep.tile([P, PASSES, BANK * FP4_WORD_BYTES], U8, name="words%d%d" % (w, f), align_bytes=64) for w, f in banks}
        planes = [keep.tile([P, PASSES, FEATURES], U8, name="planes%d" % w, align_bytes=64) for w in range(PROJECTIONS)]
        zeros = keep.tile([P, IDLE_COLUMNS], F32)
        bias_cols = [keep.tile([P, 2 * BIAS_WORDS], BF16, name="bias_cols%d" % w) for w in range(PROJECTIONS)]
        bias_all = [keep.tile([P, FEATURES // 2], F32, name="bias_all%d" % w) for w in range(PROJECTIONS)]
        ident = keep.tile([P, P], F32)
        table_warmer = keep.tile([P, 1], F32)
        grouped = keep.tile([P, PASSES, P, PACK], BF16, align_bytes=64)
        x_codes = keep.tile([P, PASSES * P], U32, align_bytes=64)
        x_planes = keep.tile([P, PASSES * P], U8, align_bytes=64)
        y = [keep.tile([P, FEATURES], F32, name="y%d" % w) for w in range(PROJECTIONS)]
        chunk_sums = [keep.tile([P, P], F32, name="chunk_sums%d" % f) for f in range(HALVES)]
        means = [keep.tile([P, P], F32, name="means%d" % b) for b in range(len(banks))]
        by_place = [keep.tile([P, CHUNK, P], F32, name="by_place%d" % f) for f in range(HALVES)]

        nc.gpsimd.memset(zeros[:], 0.0)
        nc.vector.memset(planes[0][:].bitcast(I32), 0)
        nc.vector.memset(planes[1][:].bitcast(I32), 0)

        for w, bias in enumerate((bk, bv)):
            nc.scalar.dma_start(out=bias_cols[w][:], in_=bias.rearrange("(o x) -> o x", x=2 * BIAS_WORDS))
        nc.sync.dma_start(out=x_sb[:], in_=hidden_states.rearrange("b s e -> (b s) e"))
        make_identity(nc, ident[:])
        nc.scalar.mul(out=table_warmer[:], in_=zeros[:, 0:1], mul=1.0)

        def load_scale_rows(w, r):
            rows = weight_scales[w].rearrange("g (quad r) n -> r quad g n", r=SCALE_ROWS)
            nc.sync.dma_start(out=planes[w][r:P:QUADRANT].bitcast(I32), in_=rows[r].bitcast(I32))

        def load_words(w, f):
            bank_bytes = slice(BANK * FP4_WORD_BYTES * f, BANK * FP4_WORD_BYTES * (f + 1))
            by_partition = weight_words[w].rearrange("g p b -> p g b")
            nc.sync.dma_start(out=words[w, f][:].bitcast(I32), in_=by_partition[:, :, bank_bytes].bitcast(I32))

        for r in range(SCALE_ROWS):
            load_scale_rows(0, r)
        for f in range(HALVES):
            load_words(0, f)
        load_scale_rows(1, 0)
        load_words(1, 0)
        for r in range(1, SCALE_ROWS):
            load_scale_rows(1, r)
        load_words(1, 1)

        idle_products = psum.tile([P, IDLE_COLUMNS], F32, tag="bank")
        for repeat in range(IDLE_MATMULS):
            nc.tensor.matmul(out=idle_products[:], lhsT=zeros[:, 0:P], rhs=zeros[:], start=True, stop=True)

        x_pairs = x_sb[:].bitcast(F32)
        pairs_in_pass = P * PAIRS
        turned = []
        for g in range(PASSES):
            turned_g = psum.tile([P, PAIRS, P], F32, tag="bank")
            turned.append(turned_g)
            for u in range(PAIRS):
                nc.tensor.transpose(turned_g[:, u, :], x_pairs[:, pairs_in_pass * g + u : pairs_in_pass * (g + 1) : PAIRS], ident[:])
        for g in range(PASSES):
            nc.scalar.copy(out=grouped[:, g, :, :].bitcast(F32), in_=turned[g][:].rearrange("p u s -> p s u"))
            nc.vector.quantize_mx(
                out=x_codes[:, P * g : P * (g + 1)].bitcast(FP8X4),
                scales=x_planes[:, P * g : P * (g + 1)],
                in_=grouped[:, g, :, :].rearrange("p s j -> p (s j)"),
            )

        for w in range(PROJECTIONS):
            spread = psum.tile([P, BIAS_WORDS, P], F32, tag="bank")
            bias_words = bias_cols[w][:].bitcast(F32)
            for m in range(BIAS_WORDS):
                nc.tensor.transpose(spread[:, m, :], bias_words[:, m : m + 1].to_broadcast([P, P]), ident[:])
            nc.scalar.copy(
                out=bias_all[w][:].rearrange("p (o m) -> p o m", m=BIAS_WORDS), in_=spread[:].rearrange("p m o -> p o m")
            )

        def multiply(acc, w, f, g):
            nc.tensor.matmul_mx(
                out=acc[:],
                lhsT=x_codes[:, P * g : P * (g + 1)].bitcast(FP8X4),
                lhsT_scale=x_planes[:, P * g : P * (g + 1)],
                rhs=words[w, f][:, g, :].bitcast(FP4X4),
                rhs_scale=planes[w][:, g, BANK * f : BANK * (f + 1)],
                start=(g == 0),
                stop=(g == PASSES - 1),
            )

        accs = [psum.tile([P, BANK], F32, tag="bank", name="acc%d" % b) for b in range(len(banks))]
        for b, (w, f) in enumerate(banks):
            for g in range(PASSES):
                multiply(accs[b], w, f, g)

        for b, (w, f) in enumerate(banks):
            cols = slice(BANK * f, BANK * (f + 1))
            nc.vector.tensor_tensor(out=y[w][:, cols], in0=accs[b][:], in1=bias_all[w][:].bitcast(BF16)[:, cols], op=ADD)
            nc.sync.dma_start(
                out=full_outs[w][:, BANK_HEADS * f : BANK_HEADS * (f + 1), :],
                in_=y[w][:, cols].rearrange("p (i d) -> p i d", d=P),
            )

        by_readiness = (0, 2, 1, 3)
        pieces = []
        for b in by_readiness:
            w, f = banks[b]
            heads = BANK_HEADS if f == 0 else BANK_HEADS // 2
            for first in range(0, BANK_HEADS, heads):
                by_feature = psum.tile([P, heads, P], F32, tag="bank")
                pieces.append((w, f, first, heads, by_feature))
                for i in range(heads):
                    h = BANK_HEADS * f + first + i
                    nc.tensor.transpose(by_feature[:, i, :], y[w][:, P * h : P * (h + 1)], ident[:])
        for w, f, first, heads, by_feature in pieces:
            sums = slice(CHUNKS * first, CHUNKS * (first + heads))
            if w == 0:
                nc.scalar.copy(
                    out=by_place[f][:, :, sums].rearrange("p t (i c) -> p t i c", c=CHUNKS),
                    in_=by_feature[:].rearrange("p i (c t) -> p t i c", t=CHUNK),
                )
            else:
                nc.vector.tensor_reduce(
                    out=chunk_sums[f][:, sums].rearrange("p (i c) -> p i c", c=CHUNKS),
                    in_=by_feature[:].rearrange("p i (c t) -> p i c t", t=CHUNK),
                    axis=mybir.AxisListType.X,
                    op=ADD,
                )
        for b in by_readiness:
            w, f = banks[b]
            turned_back = psum.tile([P, P], F32, tag="bank")
            if w == 0:
                for t in range(CHUNK):
                    nc.tensor.matmul(
                        out=turned_back[:], lhsT=by_place[f][:, t, :], rhs=ident[:], start=(t == 0), stop=(t == CHUNK - 1), is_transpose=True
                    )
            else:
                nc.tensor.transpose(turned_back[:], chunk_sums[f][:], ident[:])
            if b == by_readiness[-1]:
                nc.vector.tensor_scalar_mul(out=means[b][:], in0=turned_back[:], scalar1=1.0 / CHUNK)
            else:
                nc.scalar.mul(out=means[b][:], in_=turned_back[:], mul=1.0 / CHUNK)
            nc.sync.dma_start(out=mean_outs[w][:, f, :], in_=means[b][:])
